import numpy as np
import ml_dtypes

BF16 = ml_dtypes.bfloat16


def bf(x):
    return np.asarray(x, np.float32).astype(BF16)


def f32(x):
    return np.asarray(x, np.float32)


def f64(x):
    return np.asarray(x).astype(np.float64)


def striped(idx):
    return np.tile(idx.reshape(-1, 16).T, (8, 1))


T, H, D, DV, S, L, N = 4, 128, 640, 512, 4096, 2048, 8192
SCALE = 192.0 ** -0.5


def setup_inputs():
    return {"cache": f32(np.random.standard_normal((D, S))), "q": bf(np.random.standard_normal((D, T * H))), "sink": f32(8.0 + 0.5 * np.random.standard_normal((H, 1))), "offs": striped(np.concatenate([np.random.permutation(S)[:L] for _ in range(T)]))}


def reference(cache, q, sink, offs):
    idx = offs[:16].T.reshape(-1)
    res = []
    for t in range(T):
        k = f64(cache)[:, idx[t * L:(t + 1) * L]]
        z = SCALE * (f64(q)[:, t * H:(t + 1) * H].T @ k)
        m = np.maximum(z.max(axis=1, keepdims=True), f64(sink))
        e = np.exp(z - m)
        p = e / (e.sum(axis=1, keepdims=True) + np.exp(f64(sink) - m))
        res.append(k[:DV] @ p.T)
    return np.concatenate(res, axis=1)

@@ -1,0 +1,191 @@
+from contextlib import ExitStack
+
+import concourse.mybir as mybir
+from concourse.masks import make_identity
+
+T, H, D, DV, S, L = 4, 128, 640, 512, 4096, 2048
+N = T * L
+P = 128
+BLOCKS = D // P
+VALUE_BLOCKS = DV // P
+PIECE = 512
+PIECES = L // PIECE
+SUBS = PIECE // P
+SCALE = 192.0**-0.5
+
+LAG = 3
+
+FLOPS = 2 * T * H * L * (D + DV)
+
+F32 = mybir.dt.float32
+BF16 = mybir.dt.bfloat16
+U16 = mybir.dt.uint16
+COPY = mybir.ActivationFunctionType.Copy
+EXP = mybir.ActivationFunctionType.Exp
+MULT = mybir.AluOpType.mult
+MIN = mybir.AluOpType.min
+X = mybir.AxisListType.X
+
+
+def tile_deepseekv4mlaattention_b_kernel(tc, cache, q, sink, offs, out):
+    nc = tc.nc
+    with ExitStack() as ctx:
+        held = ctx.enter_context(tc.tile_pool(name="held", bufs=1))
+        ring = ctx.enter_context(tc.tile_pool(name="ring", bufs=4))
+        per_token = ctx.enter_context(tc.tile_pool(name="per_token", bufs=2))
+        score_banks = ctx.enter_context(tc.psum_pool(name="score_banks", bufs=1))
+        flip_banks = ctx.enter_context(tc.psum_pool(name="flip_banks", bufs=2))
+        out_banks = ctx.enter_context(tc.psum_pool(name="out_banks", bufs=1))
+
+        offsets = held.tile([P, N // 16], U16, name="offsets")
+        nc.sync.dma_start(offsets[:], offs)
+        cache_sb = []
+        q_sb = []
+        for b in range(BLOCKS):
+            cache_b = held.tile([P, S], F32, name=f"cache{b}")
+            nc.sync.dma_start(cache_b[:], cache[b * P : (b + 1) * P, :])
+            cache_sb.append(cache_b)
+            q_b = held.tile([P, T * H], BF16, name=f"q{b}")
+            nc.sync.dma_start(q_b[:], q[b * P : (b + 1) * P, :])
+            q_sb.append(q_b)
+        sink_sb = held.tile([P, 1], F32, name="sink_sb")
+        nc.gpsimd.dma_start(sink_sb[:], sink)
+
+        identity_bf16 = held.tile([P, P], BF16, name="identity_bf16")
+        make_identity(nc, identity_bf16[:])
+        identity_f32 = held.tile([P, P], F32, name="identity_f32")
+        make_identity(nc, identity_f32[:])
+        neg_sink = held.tile([P, 1], F32, name="neg_sink")
+        nc.vector.tensor_scalar_mul(neg_sink[:], sink_sb[:], -1.0)
+
+        tiles = {}
+
+        def pick(t, b, c):
+            if b == 0 and c == 0:
+                tiles[t] = {
+                    "picked": per_token.tile([P, BLOCKS, L], BF16, name="picked"),
+                    "values": per_token.tile([P, L // P, DV], BF16, name="values"),
+                    "piece_max": per_token.tile([P, PIECES], F32, name="piece_max"),
+                }
+            first = (t * L + c * PIECE) // 16
+            gathered = ring.tile([P, PIECE], F32, name="gathered")
+            nc.scalar.activation(
+                gathered[:],
+                cache_sb[b][:].indirect(offsets[:, first : first + PIECE // 16]),
+                COPY,
+            )
+            nc.gpsimd.tensor_copy(
+                tiles[t]["picked"][:, b, c * PIECE : (c + 1) * PIECE], gathered[:]
+            )
+
+        def score(t, b, c):
+            tok = tiles[t]
+            if b == 0:
+                tok[f"z{c}"] = score_banks.tile([P, PIECE], F32, name=f"z{c}")
+            z = tok[f"z{c}"]
+            nc.tensor.matmul(
+                z[:],
+                lhsT=q_sb[b][:, t * H : (t + 1) * H],
+                rhs=tok["picked"][:, b, c * PIECE : (c + 1) * PIECE],
+                start=(b == 0),
+                stop=(b == BLOCKS - 1),
+            )
+            if b == BLOCKS - 1:
+                nc.vector.reduce_max(tok["piece_max"][:, c : c + 1], z[:], axis=X)
+            if b < VALUE_BLOCKS:
+                flipped = flip_banks.tile([P, SUBS, P], BF16, name="flipped")
+                for i in range(SUBS):
+                    j0 = c * PIECE + i * P
+                    nc.tensor.transpose(
+                        flipped[:, i, :], tok["picked"][:, b, j0 : j0 + P], identity_bf16[:]
+                    )
+                nc.vector.tensor_copy(
+                    tok["values"][:, c * SUBS : (c + 1) * SUBS, b * P : (b + 1) * P],
+                    flipped[:],
+                )
+
+        def shift(t):
+            tok = tiles[t]
+            tok["weights"] = per_token.tile([P, L], BF16, name="weights")
+            tok["weights_t"] = per_token.tile([P, L // P, H], BF16, name="weights_t")
+            tok["sums"] = per_token.tile([P, PIECES + 1], F32, name="sums")
+            tok["neg_m"] = per_token.tile([P, 1], F32, name="neg_m")
+            tok["product"] = out_banks.tile([P, DV], F32, name="product")
+            run_max = per_token.tile([P, 1], F32, name="run_max")
+            nc.vector.reduce_max(run_max[:], tok["piece_max"][:], axis=X)
+            nc.vector.tensor_scalar(
+                tok["neg_m"][:], run_max[:], -SCALE, neg_sink[:], MULT, MIN
+            )
+            nc.scalar.activation(
+                tok["sums"][:, PIECES : PIECES + 1], sink_sb[:], EXP, bias=tok["neg_m"][:]
+            )
+
+        def weigh(t, c):
+            tok = tiles[t]
+            nc.scalar.activation(
+                tok["weights"][:, c * PIECE : (c + 1) * PIECE],
+                tok[f"z{c}"][:],
+                EXP,
+                bias=tok["neg_m"][:],
+                scale=SCALE,
+                accum_out=tok["sums"][:, c : c + 1],
+            )
+            flipped = flip_banks.tile([P, SUBS, P], BF16, name="flipped")
+            for i in range(SUBS):
+                j0 = c * PIECE + i * P
+                nc.tensor.transpose(
+                    flipped[:, i, :], tok["weights"][:, j0 : j0 + P], identity_bf16[:]
+                )
+            nc.vector.tensor_copy(tok["weights_t"][:, c * SUBS : (c + 1) * SUBS, :], flipped[:])
+
+        def mix(t, c):
+            tok = tiles[t]
+            for g in range(c * SUBS, (c + 1) * SUBS):
+                nc.tensor.matmul(
+                    tok["product"][:],
+                    lhsT=tok["weights_t"][:, g, :],
+                    rhs=tok["values"][:, g, :],
+                    start=(g == 0),
+                    stop=(g == L // P - 1),
+                )
+
+        def close(t):
+            tok = tiles[t]
+            den = per_token.tile([P, 1], F32, name="den")
+            nc.vector.reduce_sum(den[:], tok["sums"][:], axis=X)
+            inv_den = per_token.tile([P, 1], F32, name="inv_den")
+            nc.vector.reciprocal(inv_den[:], den[:])
+            normed = per_token.tile([P, DV], F32, name="normed")
+            nc.vector.tensor_scalar_mul(normed[:], tok["product"][:], inv_den[:])
+            turned = out_banks.tile([P, VALUE_BLOCKS, H], F32, name="turned")
+            for vb in range(VALUE_BLOCKS):
+                nc.tensor.transpose(
+                    turned[:, vb, :], normed[:, vb * P : (vb + 1) * P], identity_f32[:]
+                )
+            result = per_token.tile([P, VALUE_BLOCKS, H], F32, name="result")
+            nc.vector.tensor_copy(result[:], turned[:])
+            nc.sync.dma_start(
+                out.rearrange("(vb p) c -> p vb c", p=P)[:, :, t * H : (t + 1) * H], result[:]
+            )
+
+        steps = [(t, b, c) for t in range(T) for b in range(BLOCKS) for c in range(PIECES)]
+        for i in range(len(steps) + LAG):
+            if i < len(steps):
+                pick(*steps[i])
+            if i >= LAG:
+                t, b, c = steps[i - LAG]
+                after_a_token = b == 0 and t > 0
+                if after_a_token:
+                    if c == 0:
+                        shift(t - 1)
+                    weigh(t - 1, c)
+                score(t, b, c)
+                if after_a_token:
+                    mix(t - 1, c)
+                    if c == PIECES - 1:
+                        close(t - 1)
+        shift(T - 1)
+        for c in range(PIECES):
+            weigh(T - 1, c)
+            mix(T - 1, c)
+        close(T - 1)

@@ -13,8 +13,6 @@ PIECES = L // PIECE
 SUBS = PIECE // P
 SCALE = 192.0**-0.5
 
-LAG = 3
-
 FLOPS = 2 * T * H * L * (D + DV)
 
 F32 = mybir.dt.float32
@@ -23,7 +21,7 @@ U16 = mybir.dt.uint16
 COPY = mybir.ActivationFunctionType.Copy
 EXP = mybir.ActivationFunctionType.Exp
 MULT = mybir.AluOpType.mult
-MIN = mybir.AluOpType.min
+MAX = mybir.AluOpType.max
 X = mybir.AxisListType.X
 
 
@@ -39,6 +37,8 @@ def tile_deepseekv4mlaattention_b_kernel(tc, cache, q, sink, offs, out):
 
         offsets = held.tile([P, N // 16], U16, name="offsets")
         nc.sync.dma_start(offsets[:], offs)
+        sink_sb = held.tile([P, 1], F32, name="sink_sb")
+        nc.sync.dma_start(sink_sb[:], sink)
         cache_sb = []
         q_sb = []
         for b in range(BLOCKS):
@@ -48,25 +48,14 @@ def tile_deepseekv4mlaattention_b_kernel(tc, cache, q, sink, offs, out):
             q_b = held.tile([P, T * H], BF16, name=f"q{b}")
             nc.sync.dma_start(q_b[:], q[b * P : (b + 1) * P, :])
             q_sb.append(q_b)
-        sink_sb = held.tile([P, 1], F32, name="sink_sb")
-        nc.gpsimd.dma_start(sink_sb[:], sink)
-
         identity_bf16 = held.tile([P, P], BF16, name="identity_bf16")
         make_identity(nc, identity_bf16[:])
         identity_f32 = held.tile([P, P], F32, name="identity_f32")
         make_identity(nc, identity_f32[:])
-        neg_sink = held.tile([P, 1], F32, name="neg_sink")
-        nc.vector.tensor_scalar_mul(neg_sink[:], sink_sb[:], -1.0)
 
         tiles = {}
 
         def pick(t, b, c):
-            if b == 0 and c == 0:
-                tiles[t] = {
-                    "picked": per_token.tile([P, BLOCKS, L], BF16, name="picked"),
-                    "values": per_token.tile([P, L // P, DV], BF16, name="values"),
-                    "piece_max": per_token.tile([P, PIECES], F32, name="piece_max"),
-                }
             first = (t * L + c * PIECE) // 16
             gathered = ring.tile([P, PIECE], F32, name="gathered")
             nc.scalar.activation(
@@ -74,11 +63,26 @@ def tile_deepseekv4mlaattention_b_kernel(tc, cache, q, sink, offs, out):
                 cache_sb[b][:].indirect(offsets[:, first : first + PIECE // 16]),
                 COPY,
             )
-            nc.gpsimd.tensor_copy(
-                tiles[t]["picked"][:, b, c * PIECE : (c + 1) * PIECE], gathered[:]
-            )
+            picked = ring.tile([P, PIECE], BF16, name="picked")
+            nc.gpsimd.tensor_copy(picked[:], gathered[:])
+            return picked
 
-        def score(t, b, c):
+        def flip(piece, flipped_sb):
+            flipped = flip_banks.tile([P, SUBS, P], BF16, name="flipped")
+            for i in range(SUBS):
+                nc.tensor.transpose(
+                    flipped[:, i, :], piece[:, i * P : (i + 1) * P], identity_bf16[:]
+                )
+            nc.vector.tensor_copy(flipped_sb, flipped[:])
+
+        def score(t, b, c, picked):
+            if b == 0 and c == 0:
+                tiles[t] = {
+                    "values": per_token.tile([P, L // P, DV], BF16, name="values"),
+                    "scaled": per_token.tile([P, L], F32, name="scaled"),
+                    "peaks": per_token.tile([P, PIECES + 1], F32, name="peaks"),
+                }
+                nc.vector.tensor_copy(tiles[t]["peaks"][:, PIECES : PIECES + 1], sink_sb[:])
             tok = tiles[t]
             if b == 0:
                 tok[f"z{c}"] = score_banks.tile([P, PIECE], F32, name=f"z{c}")
@@ -86,67 +90,55 @@ def tile_deepseekv4mlaattention_b_kernel(tc, cache, q, sink, offs, out):
             nc.tensor.matmul(
                 z[:],
                 lhsT=q_sb[b][:, t * H : (t + 1) * H],
-                rhs=tok["picked"][:, b, c * PIECE : (c + 1) * PIECE],
+                rhs=picked[:],
                 start=(b == 0),
                 stop=(b == BLOCKS - 1),
             )
-            if b == BLOCKS - 1:
-                nc.vector.reduce_max(tok["piece_max"][:, c : c + 1], z[:], axis=X)
             if b < VALUE_BLOCKS:
-                flipped = flip_banks.tile([P, SUBS, P], BF16, name="flipped")
-                for i in range(SUBS):
-                    j0 = c * PIECE + i * P
-                    nc.tensor.transpose(
-                        flipped[:, i, :], tok["picked"][:, b, j0 : j0 + P], identity_bf16[:]
-                    )
-                nc.vector.tensor_copy(
-                    tok["values"][:, c * SUBS : (c + 1) * SUBS, b * P : (b + 1) * P],
-                    flipped[:],
+                flip(picked[:], tok["values"][:, c * SUBS : (c + 1) * SUBS, b * P : (b + 1) * P])
+            else:
+                nc.vector.tensor_scalar(
+                    tok["scaled"][:, c * PIECE : (c + 1) * PIECE],
+                    z[:],
+                    SCALE,
+                    None,
+                    MULT,
+                    MAX,
+                    accum_out=tok["peaks"][:, c : c + 1],
                 )
-
-        def shift(t):
-            tok = tiles[t]
-            tok["weights"] = per_token.tile([P, L], BF16, name="weights")
-            tok["weights_t"] = per_token.tile([P, L // P, H], BF16, name="weights_t")
-            tok["sums"] = per_token.tile([P, PIECES + 1], F32, name="sums")
-            tok["neg_m"] = per_token.tile([P, 1], F32, name="neg_m")
-            tok["product"] = out_banks.tile([P, DV], F32, name="product")
-            run_max = per_token.tile([P, 1], F32, name="run_max")
-            nc.vector.reduce_max(run_max[:], tok["piece_max"][:], axis=X)
-            nc.vector.tensor_scalar(
-                tok["neg_m"][:], run_max[:], -SCALE, neg_sink[:], MULT, MIN
-            )
-            nc.scalar.activation(
-                tok["sums"][:, PIECES : PIECES + 1], sink_sb[:], EXP, bias=tok["neg_m"][:]
-            )
 
         def weigh(t, c):
             tok = tiles[t]
+            if c == 0:
+                tok["weights"] = per_token.tile([P, L], BF16, name="weights")
+                tok["sums"] = per_token.tile([P, PIECES + 1], F32, name="sums")
+                tok["neg_m"] = per_token.tile([P, 1], F32, name="neg_m")
+                nc.vector.reduce_max(tok["neg_m"][:], tok["peaks"][:], axis=X, negate=True)
             nc.scalar.activation(
                 tok["weights"][:, c * PIECE : (c + 1) * PIECE],
-                tok[f"z{c}"][:],
+                tok["scaled"][:, c * PIECE : (c + 1) * PIECE],
                 EXP,
                 bias=tok["neg_m"][:],
-                scale=SCALE,
                 accum_out=tok["sums"][:, c : c + 1],
             )
-            flipped = flip_banks.tile([P, SUBS, P], BF16, name="flipped")
-            for i in range(SUBS):
-                j0 = c * PIECE + i * P
-                nc.tensor.transpose(
-                    flipped[:, i, :], tok["weights"][:, j0 : j0 + P], identity_bf16[:]
+            if c == PIECES - 1:
+                nc.scalar.activation(
+                    tok["sums"][:, PIECES : PIECES + 1], sink_sb[:], EXP, bias=tok["neg_m"][:]
                 )
-            nc.vector.tensor_copy(tok["weights_t"][:, c * SUBS : (c + 1) * SUBS, :], flipped[:])
 
         def mix(t, c):
             tok = tiles[t]
-            for g in range(c * SUBS, (c + 1) * SUBS):
+            if c == 0:
+                tok["product"] = out_banks.tile([P, DV], F32, name="product")
+            weights_t = ring.tile([P, SUBS, H], BF16, name="weights_t")
+            flip(tok["weights"][:, c * PIECE : (c + 1) * PIECE], weights_t[:])
+            for i in range(SUBS):
                 nc.tensor.matmul(
                     tok["product"][:],
-                    lhsT=tok["weights_t"][:, g, :],
-                    rhs=tok["values"][:, g, :],
-                    start=(g == 0),
-                    stop=(g == L // P - 1),
+                    lhsT=weights_t[:, i, :],
+                    rhs=tok["values"][:, c * SUBS + i, :],
+                    start=(c == 0 and i == 0),
+                    stop=(c == PIECES - 1 and i == SUBS - 1),
                 )
 
         def close(t):
@@ -168,24 +160,16 @@ def tile_deepseekv4mlaattention_b_kernel(tc, cache, q, sink, offs, out):
                 out.rearrange("(vb p) c -> p vb c", p=P)[:, :, t * H : (t + 1) * H], result[:]
             )
 
-        steps = [(t, b, c) for t in range(T) for b in range(BLOCKS) for c in range(PIECES)]
-        for i in range(len(steps) + LAG):
-            if i < len(steps):
-                pick(*steps[i])
-            if i >= LAG:
-                t, b, c = steps[i - LAG]
-                after_a_token = b == 0 and t > 0
-                if after_a_token:
-                    if c == 0:
-                        shift(t - 1)
-                    weigh(t - 1, c)
-                score(t, b, c)
-                if after_a_token:
-                    mix(t - 1, c)
-                    if c == PIECES - 1:
-                        close(t - 1)
-        shift(T - 1)
-        for c in range(PIECES):
-            weigh(T - 1, c)
-            mix(T - 1, c)
-        close(T - 1)
+        for t in range(T + 1):
+            for b in range(BLOCKS):
+                for c in range(PIECES):
+                    if t < T:
+                        picked = pick(t, b, c)
+                    if t > 0 and b == 0:
+                        weigh(t - 1, c)
+                    if t < T:
+                        score(t, b, c, picked)
+                    if t > 0 and b == 1:
+                        mix(t - 1, c)
+                        if c == PIECES - 1:
+                            close(t - 1)

@@ -111,6 +111,7 @@ def tile_deepseekv4mlaattention_b_kernel(tc, cache, q, sink, offs, out):
             tok = tiles[t]
             if c == 0:
                 tok["weights"] = per_token.tile([P, L], BF16, name="weights")
+                tok["weights_t"] = per_token.tile([P, L // P, H], BF16, name="weights_t")
                 tok["sums"] = per_token.tile([P, PIECES + 1], F32, name="sums")
                 tok["neg_m"] = per_token.tile([P, 1], F32, name="neg_m")
                 nc.vector.reduce_max(tok["neg_m"][:], tok["peaks"][:], axis=X, negate=True)
@@ -126,36 +127,39 @@ def tile_deepseekv4mlaattention_b_kernel(tc, cache, q, sink, offs, out):
                     tok["sums"][:, PIECES : PIECES + 1], sink_sb[:], EXP, bias=tok["neg_m"][:]
                 )
 
-        def mix(t, c):
+        def spread(t):
             tok = tiles[t]
-            if c == 0:
-                tok["product"] = out_banks.tile([P, DV], F32, name="product")
-            weights_t = ring.tile([P, SUBS, H], BF16, name="weights_t")
-            flip(tok["weights"][:, c * PIECE : (c + 1) * PIECE], weights_t[:])
-            for i in range(SUBS):
+            den = per_token.tile([P, 1], F32, name="den")
+            nc.vector.reduce_sum(den[:], tok["sums"][:], axis=X)
+            inv_den_rows = per_token.tile([P, P], F32, name="inv_den_rows")
+            nc.vector.reciprocal(inv_den_rows[:], den[:].to_broadcast([P, P]))
+            turned = out_banks.tile([P, H], F32, name="turned")
+            nc.tensor.transpose(turned[:], inv_den_rows[:], identity_f32[:])
+            tok["inv_den_columns"] = per_token.tile([P, 1, H], F32, name="inv_den_columns")
+            nc.vector.tensor_copy(tok["inv_den_columns"][:, 0, :], turned[:])
+
+        def mix(t, vb):
+            tok = tiles[t]
+            if vb == 0:
+                tok["product"] = out_banks.tile([P, VALUE_BLOCKS, H], F32, name="product")
+            for g in range(L // P):
                 nc.tensor.matmul(
-                    tok["product"][:],
-                    lhsT=weights_t[:, i, :],
-                    rhs=tok["values"][:, c * SUBS + i, :],
-                    start=(c == 0 and i == 0),
-                    stop=(c == PIECES - 1 and i == SUBS - 1),
+                    tok["product"][:, vb, :],
+                    lhsT=tok["values"][:, g, vb * P : (vb + 1) * P],
+                    rhs=tok["weights_t"][:, g, :],
+                    start=(g == 0),
+                    stop=(g == L // P - 1),
                 )
 
         def close(t):
             tok = tiles[t]
-            den = per_token.tile([P, 1], F32, name="den")
-            nc.vector.reduce_sum(den[:], tok["sums"][:], axis=X)
-            inv_den = per_token.tile([P, 1], F32, name="inv_den")
-            nc.vector.reciprocal(inv_den[:], den[:])
-            normed = per_token.tile([P, DV], F32, name="normed")
-            nc.vector.tensor_scalar_mul(normed[:], tok["product"][:], inv_den[:])
-            turned = out_banks.tile([P, VALUE_BLOCKS, H], F32, name="turned")
-            for vb in range(VALUE_BLOCKS):
-                nc.tensor.transpose(
-                    turned[:, vb, :], normed[:, vb * P : (vb + 1) * P], identity_f32[:]
-                )
             result = per_token.tile([P, VALUE_BLOCKS, H], F32, name="result")
-            nc.vector.tensor_copy(result[:], turned[:])
+            nc.vector.tensor_tensor(
+                result[:],
+                tok["product"][:],
+                tok["inv_den_columns"][:].to_broadcast([P, VALUE_BLOCKS, H]),
+                MULT,
+            )
             nc.sync.dma_start(
                 out.rearrange("(vb p) c -> p vb c", p=P)[:, :, t * H : (t + 1) * H], result[:]
             )
@@ -170,6 +174,13 @@ def tile_deepseekv4mlaattention_b_kernel(tc, cache, q, sink, offs, out):
                     if t < T:
                         score(t, b, c, picked)
                     if t > 0 and b == 1:
-                        mix(t - 1, c)
+                        flip(
+                            tiles[t - 1]["weights"][:, c * PIECE : (c + 1) * PIECE],
+                            tiles[t - 1]["weights_t"][:, c * SUBS : (c + 1) * SUBS, :],
+                        )
                         if c == PIECES - 1:
+                            spread(t - 1)
+                    if t > 0 and b == 2:
+                        mix(t - 1, c)
+                        if c == VALUE_BLOCKS - 1:
                             close(t - 1)

@@ -29,11 +29,17 @@ def tile_deepseekv4mlaattention_b_kernel(tc, cache, q, sink, offs, out):
     nc = tc.nc
     with ExitStack() as ctx:
         held = ctx.enter_context(tc.tile_pool(name="held", bufs=1))
+        run_ring = ctx.enter_context(tc.tile_pool(name="run_ring", bufs=2))
         ring = ctx.enter_context(tc.tile_pool(name="ring", bufs=4))
         per_token = ctx.enter_context(tc.tile_pool(name="per_token", bufs=2))
         score_banks = ctx.enter_context(tc.psum_pool(name="score_banks", bufs=1))
         flip_banks = ctx.enter_context(tc.psum_pool(name="flip_banks", bufs=2))
         out_banks = ctx.enter_context(tc.psum_pool(name="out_banks", bufs=1))
+
+        zero = held.tile([P, 1], F32, name="zero")
+        nc.vector.memset(zero[:], 0.0)
+        one = held.tile([P, 1], F32, name="one")
+        nc.scalar.activation(one[:], zero[:], EXP)
 
         offsets = held.tile([P, N // 16], U16, name="offsets")
         nc.sync.dma_start(offsets[:], offs)
@@ -55,16 +61,19 @@ def tile_deepseekv4mlaattention_b_kernel(tc, cache, q, sink, offs, out):
 
         tiles = {}
 
-        def pick(t, b, c):
-            first = (t * L + c * PIECE) // 16
-            gathered = ring.tile([P, PIECE], F32, name="gathered")
+        def gather(t, b):
+            first = t * L // 16
+            gathered = run_ring.tile([P, L], F32, name="gathered")
             nc.scalar.activation(
                 gathered[:],
-                cache_sb[b][:].indirect(offsets[:, first : first + PIECE // 16]),
+                cache_sb[b][:].indirect(offsets[:, first : first + L // 16]),
                 COPY,
             )
+            return gathered
+
+        def rounded(gathered, c):
             picked = ring.tile([P, PIECE], BF16, name="picked")
-            nc.gpsimd.tensor_copy(picked[:], gathered[:])
+            nc.gpsimd.tensor_copy(picked[:], gathered[:, c * PIECE : (c + 1) * PIECE])
             return picked
 
         def flip(piece, flipped_sb):
@@ -166,21 +175,20 @@ def tile_deepseekv4mlaattention_b_kernel(tc, cache, q, sink, offs, out):
 
         for t in range(T + 1):
             for b in range(BLOCKS):
+                if t < T:
+                    gathered = gather(t, b)
                 for c in range(PIECES):
-                    if t < T:
-                        picked = pick(t, b, c)
                     if t > 0 and b == 0:
                         weigh(t - 1, c)
                     if t < T:
-                        score(t, b, c, picked)
+                        score(t, b, c, rounded(gathered, c))
                     if t > 0 and b == 1:
                         flip(
                             tiles[t - 1]["weights"][:, c * PIECE : (c + 1) * PIECE],
                             tiles[t - 1]["weights_t"][:, c * SUBS : (c + 1) * SUBS, :],
                         )
-                        if c == PIECES - 1:
-                            spread(t - 1)
-                    if t > 0 and b == 2:
-                        mix(t - 1, c)
-                        if c == VALUE_BLOCKS - 1:
-                            close(t - 1)
+                if t > 0 and b == 1:
+                    spread(t - 1)
+                    for vb in range(VALUE_BLOCKS):
+                        mix(t - 1, vb)
+                    close(t - 1)

@@ -43,17 +43,15 @@ def tile_deepseekv4mlaattention_b_kernel(tc, cache, q, sink, offs, out):
 
         offsets = held.tile([P, N // 16], U16, name="offsets")
         nc.sync.dma_start(offsets[:], offs)
+        cache_sb = [held.tile([P, S], F32, name=f"cache{b}") for b in range(BLOCKS)]
+        q_sb = [held.tile([P, T * H], BF16, name=f"q{b}") for b in range(BLOCKS)]
+        for b in range(BLOCKS + 1):
+            if b < BLOCKS:
+                nc.sync.dma_start(cache_sb[b][:], cache[b * P : (b + 1) * P, :])
+            if b > 0:
+                nc.sync.dma_start(q_sb[b - 1][:], q[(b - 1) * P : b * P, :])
         sink_sb = held.tile([P, 1], F32, name="sink_sb")
         nc.sync.dma_start(sink_sb[:], sink)
-        cache_sb = []
-        q_sb = []
-        for b in range(BLOCKS):
-            cache_b = held.tile([P, S], F32, name=f"cache{b}")
-            nc.sync.dma_start(cache_b[:], cache[b * P : (b + 1) * P, :])
-            cache_sb.append(cache_b)
-            q_b = held.tile([P, T * H], BF16, name=f"q{b}")
-            nc.sync.dma_start(q_b[:], q[b * P : (b + 1) * P, :])
-            q_sb.append(q_b)
         identity_bf16 = held.tile([P, P], BF16, name="identity_bf16")
         make_identity(nc, identity_bf16[:])
         identity_f32 = held.tile([P, P], F32, name="identity_f32")
@@ -71,9 +69,11 @@ def tile_deepseekv4mlaattention_b_kernel(tc, cache, q, sink, offs, out):
             )
             return gathered
 
-        def rounded(gathered, c):
+        def rounded(gathered, b, c):
             picked = ring.tile([P, PIECE], BF16, name="picked")
-            nc.gpsimd.tensor_copy(picked[:], gathered[:, c * PIECE : (c + 1) * PIECE])
+            helped = b == BLOCKS - 1 and c == PIECES - 1
+            engine = nc.vector if helped else nc.gpsimd
+            engine.tensor_copy(picked[:], gathered[:, c * PIECE : (c + 1) * PIECE])
             return picked
 
         def flip(piece, flipped_sb):
@@ -181,7 +181,7 @@ def tile_deepseekv4mlaattention_b_kernel(tc, cache, q, sink, offs, out):
                     if t > 0 and b == 0:
                         weigh(t - 1, c)
                     if t < T:
-                        score(t, b, c, rounded(gathered, c))
+                        score(t, b, c, rounded(gathered, b, c))
                     if t > 0 and b == 1:
                         flip(
                             tiles[t - 1]["weights"][:, c * PIECE : (c + 1) * PIECE],

@@ -69,11 +69,9 @@ def tile_deepseekv4mlaattention_b_kernel(tc, cache, q, sink, offs, out):
             )
             return gathered
 
-        def rounded(gathered, b, c):
+        def rounded(gathered, c):
             picked = ring.tile([P, PIECE], BF16, name="picked")
-            helped = b == BLOCKS - 1 and c == PIECES - 1
-            engine = nc.vector if helped else nc.gpsimd
-            engine.tensor_copy(picked[:], gathered[:, c * PIECE : (c + 1) * PIECE])
+            nc.gpsimd.tensor_copy(picked[:], gathered[:, c * PIECE : (c + 1) * PIECE])
             return picked
 
         def flip(piece, flipped_sb):
@@ -181,7 +179,7 @@ def tile_deepseekv4mlaattention_b_kernel(tc, cache, q, sink, offs, out):
                     if t > 0 and b == 0:
                         weigh(t - 1, c)
                     if t < T:
-                        score(t, b, c, rounded(gathered, b, c))
+                        score(t, b, c, rounded(gathered, c))
                     if t > 0 and b == 1:
                         flip(
                             tiles[t - 1]["weights"][:, c * PIECE : (c + 1) * PIECE],

@@ -59,14 +59,15 @@ def tile_deepseekv4mlaattention_b_kernel(tc, cache, q, sink, offs, out):
 
         tiles = {}
 
-        def gather(t, b):
-            first = t * L // 16
+        def gather(t, b, width):
             gathered = run_ring.tile([P, L], F32, name="gathered")
-            nc.scalar.activation(
-                gathered[:],
-                cache_sb[b][:].indirect(offsets[:, first : first + L // 16]),
-                COPY,
-            )
+            for j in range(0, L, width):
+                first = (t * L + j) // 16
+                nc.scalar.activation(
+                    gathered[:, j : j + width],
+                    cache_sb[b][:].indirect(offsets[:, first : first + width // 16]),
+                    COPY,
+                )
             return gathered
 
         def rounded(gathered, c):
@@ -92,7 +93,7 @@ def tile_deepseekv4mlaattention_b_kernel(tc, cache, q, sink, offs, out):
                 nc.vector.tensor_copy(tiles[t]["peaks"][:, PIECES : PIECES + 1], sink_sb[:])
             tok = tiles[t]
             if b == 0:
-                tok[f"z{c}"] = score_banks.tile([P, PIECE], F32, name=f"z{c}")
+                tok[f"z{c}"] = score_banks.tile([P, PIECE], F32, name=f"z{c}", tag=f"bank{c}")
             z = tok[f"z{c}"]
             nc.tensor.matmul(
                 z[:],
@@ -114,24 +115,27 @@ def tile_deepseekv4mlaattention_b_kernel(tc, cache, q, sink, offs, out):
                     accum_out=tok["peaks"][:, c : c + 1],
                 )
 
-        def weigh(t, c):
+        def weigh(t, c, pieces):
             tok = tiles[t]
             if c == 0:
                 tok["weights"] = per_token.tile([P, L], BF16, name="weights")
                 tok["weights_t"] = per_token.tile([P, L // P, H], BF16, name="weights_t")
-                tok["sums"] = per_token.tile([P, PIECES + 1], F32, name="sums")
+                tok["sums"] = per_token.tile([P, PIECES // pieces + 1], F32, name="sums")
                 tok["neg_m"] = per_token.tile([P, 1], F32, name="neg_m")
                 nc.vector.reduce_max(tok["neg_m"][:], tok["peaks"][:], axis=X, negate=True)
             nc.scalar.activation(
-                tok["weights"][:, c * PIECE : (c + 1) * PIECE],
-                tok["scaled"][:, c * PIECE : (c + 1) * PIECE],
+                tok["weights"][:, c * PIECE : (c + pieces) * PIECE],
+                tok["scaled"][:, c * PIECE : (c + pieces) * PIECE],
                 EXP,
                 bias=tok["neg_m"][:],
-                accum_out=tok["sums"][:, c : c + 1],
+                accum_out=tok["sums"][:, c // pieces : c // pieces + 1],
             )
-            if c == PIECES - 1:
+            if c + pieces == PIECES:
                 nc.scalar.activation(
-                    tok["sums"][:, PIECES : PIECES + 1], sink_sb[:], EXP, bias=tok["neg_m"][:]
+                    tok["sums"][:, PIECES // pieces : PIECES // pieces + 1],
+                    sink_sb[:],
+                    EXP,
+                    bias=tok["neg_m"][:],
                 )
 
         def spread(t):
@@ -145,13 +149,11 @@ def tile_deepseekv4mlaattention_b_kernel(tc, cache, q, sink, offs, out):
             tok["inv_den_columns"] = per_token.tile([P, 1, H], F32, name="inv_den_columns")
             nc.vector.tensor_copy(tok["inv_den_columns"][:, 0, :], turned[:])
 
-        def mix(t, vb):
+        def mix(t, vb, c):
             tok = tiles[t]
-            if vb == 0:
-                tok["product"] = out_banks.tile([P, VALUE_BLOCKS, H], F32, name="product")
-            for g in range(L // P):
+            for g in range(c * SUBS, (c + 1) * SUBS):
                 nc.tensor.matmul(
-                    tok["product"][:, vb, :],
+                    tok["products"][vb],
                     lhsT=tok["values"][:, g, vb * P : (vb + 1) * P],
                     rhs=tok["weights_t"][:, g, :],
                     start=(g == 0),
@@ -161,32 +163,51 @@ def tile_deepseekv4mlaattention_b_kernel(tc, cache, q, sink, offs, out):
         def close(t):
             tok = tiles[t]
             result = per_token.tile([P, VALUE_BLOCKS, H], F32, name="result")
-            nc.vector.tensor_tensor(
-                result[:],
-                tok["product"][:],
-                tok["inv_den_columns"][:].to_broadcast([P, VALUE_BLOCKS, H]),
-                MULT,
-            )
+            for vb in range(VALUE_BLOCKS):
+                nc.vector.tensor_tensor(
+                    result[:, vb, :], tok["products"][vb], tok["inv_den_columns"][:, 0, :], MULT
+                )
             nc.sync.dma_start(
                 out.rearrange("(vb p) c -> p vb c", p=P)[:, :, t * H : (t + 1) * H], result[:]
             )
 
-        for t in range(T + 1):
+        def flip_weights(t, c):
+            flip(
+                tiles[t]["weights"][:, c * PIECE : (c + 1) * PIECE],
+                tiles[t]["weights_t"][:, c * SUBS : (c + 1) * SUBS, :],
+            )
+
+        for t in range(T):
             for b in range(BLOCKS):
-                if t < T:
-                    gathered = gather(t, b)
+                last_gather = t == T - 1 and b == BLOCKS - 1
+                gathered = gather(t, b, PIECE if last_gather else L)
+                if t > 0 and b == 0:
+                    weigh(t - 1, 0, PIECES)
                 for c in range(PIECES):
-                    if t > 0 and b == 0:
-                        weigh(t - 1, c)
-                    if t < T:
-                        score(t, b, c, rounded(gathered, c))
+                    score(t, b, c, rounded(gathered, c))
                     if t > 0 and b == 1:
-                        flip(
-                            tiles[t - 1]["weights"][:, c * PIECE : (c + 1) * PIECE],
-                            tiles[t - 1]["weights_t"][:, c * SUBS : (c + 1) * SUBS, :],
-                        )
+                        flip_weights(t - 1, c)
                 if t > 0 and b == 1:
                     spread(t - 1)
+                    product = out_banks.tile([P, VALUE_BLOCKS, H], F32, name="product")
+                    tiles[t - 1]["products"] = [product[:, vb, :] for vb in range(VALUE_BLOCKS)]
                     for vb in range(VALUE_BLOCKS):
-                        mix(t - 1, vb)
+                        for c in range(PIECES):
+                            mix(t - 1, vb, c)
                     close(t - 1)
+
+        last = T - 1
+        for c in range(PIECES):
+            weigh(last, c, 1)
+        spread(last)
+        tiles[last]["products"] = [
+            score_banks.tile([P, H], F32, name=f"product{vb}", tag=f"bank{vb}")[:]
+            for vb in range(VALUE_BLOCKS)
+        ]
+        for c in range(PIECES + 1):
+            if c < PIECES:
+                flip_weights(last, c)
+            if c > 0:
+                for vb in range(VALUE_BLOCKS):
+                    mix(last, vb, c - 1)
+        close(last)

@@ -167,9 +167,9 @@ def tile_deepseekv4mlaattention_b_kernel(tc, cache, q, sink, offs, out):
                 nc.vector.tensor_tensor(
                     result[:, vb, :], tok["products"][vb], tok["inv_den_columns"][:, 0, :], MULT
                 )
-            nc.sync.dma_start(
-                out.rearrange("(vb p) c -> p vb c", p=P)[:, :, t * H : (t + 1) * H], result[:]
-            )
+                nc.sync.dma_start(
+                    out[vb * P : (vb + 1) * P, t * H : (t + 1) * H], result[:, vb, :]
+                )
 
         def flip_weights(t, c):
             flip(

from contextlib import ExitStack

import concourse.mybir as mybir
from concourse.masks import make_identity

T, H, D, DV, S, L = 4, 128, 640, 512, 4096, 2048
N = T * L
P = 128
BLOCKS = D // P
VALUE_BLOCKS = DV // P
PIECE = 512
PIECES = L // PIECE
SUBS = PIECE // P
SCALE = 192.0**-0.5

FLOPS = 2 * T * H * L * (D + DV)

F32 = mybir.dt.float32
BF16 = mybir.dt.bfloat16
U16 = mybir.dt.uint16
COPY = mybir.ActivationFunctionType.Copy
EXP = mybir.ActivationFunctionType.Exp
MULT = mybir.AluOpType.mult
MAX = mybir.AluOpType.max
X = mybir.AxisListType.X


def tile_deepseekv4mlaattention_b_kernel(tc, cache, q, sink, offs, out):
    nc = tc.nc
    with ExitStack() as ctx:
        held = ctx.enter_context(tc.tile_pool(name="held", bufs=1))
        run_ring = ctx.enter_context(tc.tile_pool(name="run_ring", bufs=2))
        ring = ctx.enter_context(tc.tile_pool(name="ring", bufs=4))
        per_token = ctx.enter_context(tc.tile_pool(name="per_token", bufs=2))
        score_banks = ctx.enter_context(tc.psum_pool(name="score_banks", bufs=1))
        flip_banks = ctx.enter_context(tc.psum_pool(name="flip_banks", bufs=2))
        out_banks = ctx.enter_context(tc.psum_pool(name="out_banks", bufs=1))

        zero = held.tile([P, 1], F32, name="zero")
        nc.vector.memset(zero[:], 0.0)
        one = held.tile([P, 1], F32, name="one")
        nc.scalar.activation(one[:], zero[:], EXP)

        offsets = held.tile([P, N // 16], U16, name="offsets")
        nc.sync.dma_start(offsets[:], offs)
        cache_sb = [held.tile([P, S], F32, name=f"cache{b}") for b in range(BLOCKS)]
        q_sb = [held.tile([P, T * H], BF16, name=f"q{b}") for b in range(BLOCKS)]
        for b in range(BLOCKS + 1):
            if b < BLOCKS:
                nc.sync.dma_start(cache_sb[b][:], cache[b * P : (b + 1) * P, :])
            if b > 0:
                nc.sync.dma_start(q_sb[b - 1][:], q[(b - 1) * P : b * P, :])
        sink_sb = held.tile([P, 1], F32, name="sink_sb")
        nc.sync.dma_start(sink_sb[:], sink)
        identity_bf16 = held.tile([P, P], BF16, name="identity_bf16")
        make_identity(nc, identity_bf16[:])
        identity_f32 = held.tile([P, P], F32, name="identity_f32")
        make_identity(nc, identity_f32[:])

        tiles = {}

        def gather(t, b, width):
            gathered = run_ring.tile([P, L], F32, name="gathered")
            for j in range(0, L, width):
                first = (t * L + j) // 16
                nc.scalar.activation(
                    gathered[:, j : j + width],
                    cache_sb[b][:].indirect(offsets[:, first : first + width // 16]),
                    COPY,
                )
            return gathered

        def rounded(gathered, c):
            picked = ring.tile([P, PIECE], BF16, name="picked")
            nc.gpsimd.tensor_copy(picked[:], gathered[:, c * PIECE : (c + 1) * PIECE])
            return picked

        def flip(piece, flipped_sb):
            flipped = flip_banks.tile([P, SUBS, P], BF16, name="flipped")
            for i in range(SUBS):
                nc.tensor.transpose(
                    flipped[:, i, :], piece[:, i * P : (i + 1) * P], identity_bf16[:]
                )
            nc.vector.tensor_copy(flipped_sb, flipped[:])

        def score(t, b, c, picked):
            if b == 0 and c == 0:
                tiles[t] = {
                    "values": per_token.tile([P, L // P, DV], BF16, name="values"),
                    "scaled": per_token.tile([P, L], F32, name="scaled"),
                    "peaks": per_token.tile([P, PIECES + 1], F32, name="peaks"),
                }
                nc.vector.tensor_copy(tiles[t]["peaks"][:, PIECES : PIECES + 1], sink_sb[:])
            tok = tiles[t]
            if b == 0:
                tok[f"z{c}"] = score_banks.tile([P, PIECE], F32, name=f"z{c}", tag=f"bank{c}")
            z = tok[f"z{c}"]
            nc.tensor.matmul(
                z[:],
                lhsT=q_sb[b][:, t * H : (t + 1) * H],
                rhs=picked[:],
                start=(b == 0),
                stop=(b == BLOCKS - 1),
            )
            if b < VALUE_BLOCKS:
                flip(picked[:], tok["values"][:, c * SUBS : (c + 1) * SUBS, b * P : (b + 1) * P])
            else:
                nc.vector.tensor_scalar(
                    tok["scaled"][:, c * PIECE : (c + 1) * PIECE],
                    z[:],
                    SCALE,
                    None,
                    MULT,
                    MAX,
                    accum_out=tok["peaks"][:, c : c + 1],
                )

        def weigh(t, c, pieces):
            tok = tiles[t]
            if c == 0:
                tok["weights"] = per_token.tile([P, L], BF16, name="weights")
                tok["weights_t"] = per_token.tile([P, L // P, H], BF16, name="weights_t")
                tok["sums"] = per_token.tile([P, PIECES // pieces + 1], F32, name="sums")
                tok["neg_m"] = per_token.tile([P, 1], F32, name="neg_m")
                nc.vector.reduce_max(tok["neg_m"][:], tok["peaks"][:], axis=X, negate=True)
            nc.scalar.activation(
                tok["weights"][:, c * PIECE : (c + pieces) * PIECE],
                tok["scaled"][:, c * PIECE : (c + pieces) * PIECE],
                EXP,
                bias=tok["neg_m"][:],
                accum_out=tok["sums"][:, c // pieces : c // pieces + 1],
            )
            if c + pieces == PIECES:
                nc.scalar.activation(
                    tok["sums"][:, PIECES // pieces : PIECES // pieces + 1],
                    sink_sb[:],
                    EXP,
                    bias=tok["neg_m"][:],
                )

        def spread(t):
            tok = tiles[t]
            den = per_token.tile([P, 1], F32, name="den")
            nc.vector.reduce_sum(den[:], tok["sums"][:], axis=X)
            inv_den_rows = per_token.tile([P, P], F32, name="inv_den_rows")
            nc.vector.reciprocal(inv_den_rows[:], den[:].to_broadcast([P, P]))
            turned = out_banks.tile([P, H], F32, name="turned")
            nc.tensor.transpose(turned[:], inv_den_rows[:], identity_f32[:])
            tok["inv_den_columns"] = per_token.tile([P, 1, H], F32, name="inv_den_columns")
            nc.vector.tensor_copy(tok["inv_den_columns"][:, 0, :], turned[:])

        def mix(t, vb, c):
            tok = tiles[t]
            for g in range(c * SUBS, (c + 1) * SUBS):
                nc.tensor.matmul(
                    tok["products"][vb],
                    lhsT=tok["values"][:, g, vb * P : (vb + 1) * P],
                    rhs=tok["weights_t"][:, g, :],
                    start=(g == 0),
                    stop=(g == L // P - 1),
                )

        def close(t):
            tok = tiles[t]
            result = per_token.tile([P, VALUE_BLOCKS, H], F32, name="result")
            for vb in range(VALUE_BLOCKS):
                nc.vector.tensor_tensor(
                    result[:, vb, :], tok["products"][vb], tok["inv_den_columns"][:, 0, :], MULT
                )
                nc.sync.dma_start(
                    out[vb * P : (vb + 1) * P, t * H : (t + 1) * H], result[:, vb, :]
                )

        def flip_weights(t, c):
            flip(
                tiles[t]["weights"][:, c * PIECE : (c + 1) * PIECE],
                tiles[t]["weights_t"][:, c * SUBS : (c + 1) * SUBS, :],
            )

        for t in range(T):
            for b in range(BLOCKS):
                last_gather = t == T - 1 and b == BLOCKS - 1
                gathered = gather(t, b, PIECE if last_gather else L)
                if t > 0 and b == 0:
                    weigh(t - 1, 0, PIECES)
                for c in range(PIECES):
                    score(t, b, c, rounded(gathered, c))
                    if t > 0 and b == 1:
                        flip_weights(t - 1, c)
                if t > 0 and b == 1:
                    spread(t - 1)
                    product = out_banks.tile([P, VALUE_BLOCKS, H], F32, name="product")
                    tiles[t - 1]["products"] = [product[:, vb, :] for vb in range(VALUE_BLOCKS)]
                    for vb in range(VALUE_BLOCKS):
                        for c in range(PIECES):
                            mix(t - 1, vb, c)
                    close(t - 1)

        last = T - 1
        for c in range(PIECES):
            weigh(last, c, 1)
        spread(last)
        tiles[last]["products"] = [
            score_banks.tile([P, H], F32, name=f"product{vb}", tag=f"bank{vb}")[:]
            for vb in range(VALUE_BLOCKS)
        ]
        for c in range(PIECES + 1):
            if c < PIECES:
                flip_weights(last, c)
            if c > 0:
                for vb in range(VALUE_BLOCKS):
                    mix(last, vb, c - 1)
        close(last)
